import numpy as np
import ml_dtypes


def mxq(x, axis, fmt="e4m3"):
    dtype, down = {"e4m3": (ml_dtypes.float8_e4m3fn, 7), "e5m2": (ml_dtypes.float8_e5m2, 14)}[fmt]
    v = np.moveaxis(np.asarray(x, np.float32).astype(ml_dtypes.bfloat16).astype(np.float64), axis, -1)
    blocks = v.reshape(v.shape[:-1] + (-1, 32))
    amax = np.abs(blocks).max(-1, keepdims=True)
    byte = np.maximum(np.where(amax > 0, np.frexp(amax)[1] - 1 + 127, 0) - down, 1)
    scale = np.exp2(byte - 127.0)
    codes = (blocks / scale).astype(np.float32).astype(dtype).astype(np.float64)
    return np.moveaxis((codes * scale).reshape(v.shape), -1, axis)


WIDE = False


def mx_kscale(k):
    if not WIDE:
        return np.ones(k)
    levels = np.array([10, -10, 5, -5, 0])
    a = np.random.permutation(np.resize(levels, k // 512 * 4)).reshape(k // 512, 4)
    idx = np.arange(k)
    return np.exp2(a[idx // 512, idx % 128 // 32])


BF16 = ml_dtypes.bfloat16


def bf(x):
    return np.asarray(x, np.float32).astype(BF16)


def f64(x):
    return np.asarray(x).astype(np.float64)


E2M1 = np.array([0.0, 0.5, 1.0, 1.5, 2.0, 3.0, 4.0, 6.0, -0.0, -0.5, -1.0, -1.5, -2.0, -3.0, -4.0, -6.0])


def pack_weight(w, fmt):
    k, n = w.shape
    w = f64(bf(w)).reshape(k // 32, 32, n)
    amax = np.abs(w).max(1)
    if fmt == "e4m3":
        byte = np.frexp(amax)[1] - 1 + 127 - 7
    else:
        mant, ex = np.frexp(amax / 6.0)
        byte = np.where(mant > 0.5, ex, ex - 1) + 127
    byte = np.clip(np.where(amax > 0, byte, 1), 1, 254)
    scaled = (w * np.exp2(127.0 - byte)[:, None, :]).reshape(k, n).astype(np.float32)
    by_word = np.ascontiguousarray(scaled.reshape(k // 512, 128, 4, n).transpose(0, 1, 3, 2))
    if fmt == "e4m3":
        words = by_word.astype(ml_dtypes.float8_e4m3fn).view(np.uint8)
    else:
        c = by_word.astype(ml_dtypes.float4_e2m1fn).view(np.uint8) & 0xF
        words = c[..., 0::2] | (c[..., 1::2] << 4)
    return np.ascontiguousarray(words), np.ascontiguousarray(byte.astype(np.uint8).reshape(k // 512, 16, n))


def unpack_weight(words, scales, fmt):
    g, p, n, _ = words.shape
    if fmt == "e4m3":
        vals = np.ascontiguousarray(words).view(ml_dtypes.float8_e4m3fn).astype(np.float64)
    else:
        nib = np.empty((g, p, n, 4), np.uint8)
        nib[..., 0::2] = words & 0xF
        nib[..., 1::2] = words >> 4
        vals = E2M1[nib]
    vals = vals * np.repeat(np.exp2(scales.astype(np.float64) - 127.0), 8, axis=1)[..., None]
    return vals.transpose(0, 1, 3, 2).reshape(g * 512, n)

def pack4(w):
    words, scales = pack_weight(w, "e2m1")
    return words.reshape(words.shape[0], 128, -1), scales


def unpack4(words, scales):
    return unpack_weight(words.reshape(words.shape[0], 128, -1, 2), scales, "e2m1")


T, HS, WS, WT, WH, WW, NH, HD, VID_DIM, TXT_DIM, TXT_LEN = 8, 32, 32, 8, 8, 8, 2, 64, 1024, 1536, 256
EPS = 1e-6
L_VID = T * HS * WS
N_WIN = (T // WT) * (HS // WH) * (WS // WW)
WIN_LEN = WT * WH * WW
INNER = NH * HD


def rmsnorm(x, gain):
    return x * (1.0 / np.sqrt(np.mean(x * x, axis=-1, keepdims=True) + EPS)) * gain


def window_partition(x):
    x = x.reshape(T // WT, WT, HS // WH, WH, WS // WW, WW, NH, HD)
    x = x.transpose(0, 2, 4, 1, 3, 5, 6, 7)
    return x.reshape(N_WIN, WIN_LEN, NH, HD)


def setup_inputs():
    s = mx_kscale(VID_DIM)
    vid = bf(np.random.standard_normal((L_VID, VID_DIM)) * s)
    words, scales = pack4(np.random.standard_normal((VID_DIM, 3 * INNER)) / np.sqrt(VID_DIM) / s[:, None])
    return {
        "vid": vid,
        "Wqkv_vid_words": words,
        "Wqkv_vid_scales": scales,
        "bqkv_vid": bf(0.1 * np.random.standard_normal(3 * INNER)),
        "q_scale_vid": bf(1.0 + 0.1 * np.random.standard_normal(HD)),
        "k_scale_vid": bf(1.0 + 0.1 * np.random.standard_normal(HD)),
    }


def reference(vid, Wqkv_vid_words, Wqkv_vid_scales, bqkv_vid, q_scale_vid, k_scale_vid):
    qkv = ((mxq(f64(vid), 1, "e4m3") @ unpack4(Wqkv_vid_words, Wqkv_vid_scales)) + f64(bqkv_vid)).reshape(L_VID, 3, NH, HD)
    q = rmsnorm(qkv[:, 0], f64(q_scale_vid))
    k = rmsnorm(qkv[:, 1], f64(k_scale_vid))
    return window_partition(q), window_partition(k), window_partition(qkv[:, 2])

@@ -1,0 +1,182 @@
+from contextlib import ExitStack
+
+import concourse.mybir as mybir
+from concourse.masks import make_identity
+
+F32 = mybir.dt.float32
+BF16 = mybir.dt.bfloat16
+I32 = mybir.dt.int32
+U32 = mybir.dt.uint32
+U8 = mybir.dt.uint8
+FP8X4 = mybir.dt.float8_e4m3fn_x4
+FP4X4 = mybir.dt.float4_e2m1fn_x4
+ACT = mybir.ActivationFunctionType
+ALU = mybir.AluOpType
+
+P = 128
+K = 1024
+K_PASS = 512
+PASSES = K // K_PASS
+HEADS = 2
+HEAD_DIM = 64
+INNER = HEADS * HEAD_DIM
+QKV = 3
+EPS = 1e-6
+
+FRAMES = 8
+WINDOWS = 16
+WIN_SIDE = 8
+TOKENS = FRAMES * WINDOWS * WIN_SIDE * WIN_SIDE
+
+ROUND = 4
+ROUNDS_PER_FRAME = WIN_SIDE // ROUND
+ROUNDS = FRAMES * ROUNDS_PER_FRAME
+LEAD = 6
+
+FLOPS = 2 * TOKENS * K * QKV * INNER
+
+
+def tile_naswinattention_pa_t_kernel(
+    tc, vid, Wqkv_vid_words, Wqkv_vid_scales, bqkv_vid, q_scale_vid, k_scale_vid, out_0, out_1, out_2
+):
+    nc = tc.nc
+
+    vid_by_frame = vid.rearrange("(t p j) k -> t p (j k)", t=FRAMES, p=P, j=WIN_SIDE)
+    outs_by_frame = [
+        o.rearrange("n (t l j) h f -> t n l (j h f)", t=FRAMES, l=WIN_SIDE, j=WIN_SIDE) for o in (out_0, out_1, out_2)
+    ]
+
+    with ExitStack() as stack:
+        const = stack.enter_context(tc.tile_pool(name="const", bufs=1))
+        x_pool = stack.enter_context(tc.tile_pool(name="x_pool", bufs=LEAD))
+        grouped_pool = stack.enter_context(tc.tile_pool(name="grouped_pool", bufs=2))
+        code_pool = stack.enter_context(tc.tile_pool(name="code_pool", bufs=3))
+        y_pool = stack.enter_context(tc.tile_pool(name="y_pool", bufs=4))
+        stat_pool = stack.enter_context(tc.tile_pool(name="stat_pool", bufs=4))
+        xt_psum = stack.enter_context(tc.psum_pool(name="xt_psum", bufs=4))
+        acc_psum = stack.enter_context(tc.psum_pool(name="acc_psum", bufs=4))
+
+        stack.enter_context(tc.manual_schedule())
+
+        x_of = {}
+        grouped_of = {}
+        codes_of = {}
+        y_of = {}
+
+        def load_round(r):
+            frame, part = divmod(r, ROUNDS_PER_FRAME)
+            x = x_pool.tile([P, ROUND * K], BF16, name="x")
+            nc.sync.dma_start(out=x[:], in_=vid_by_frame[frame, :, part * ROUND * K : (part + 1) * ROUND * K])
+            x_of[r] = x
+
+        load_round(0)
+
+        w_words = const.tile([P, PASSES, 2 * QKV * INNER], U8, name="w_words", align_bytes=64)
+        nc.sync.dma_start(out=w_words[:].bitcast(I32), in_=Wqkv_vid_words.bitcast(I32).rearrange("g p n -> p g n"))
+        w_scales = const.tile([P, PASSES, QKV * INNER], U8, name="w_scales", align_bytes=64)
+        nc.vector.memset(w_scales[:].bitcast(I32), 0)
+        for quadrant in range(4):
+            nc.sync.dma_start(
+                out=w_scales[32 * quadrant : 32 * quadrant + 4].bitcast(I32),
+                in_=Wqkv_vid_scales.bitcast(I32)[:, 4 * quadrant : 4 * quadrant + 4, :].rearrange("g r n -> r g n"),
+            )
+        bias = const.tile([P, QKV, INNER], BF16, name="bias")
+        nc.scalar.dma_start(out=bias[:].rearrange("p c f -> p (c f)"), in_=bqkv_vid.partition_broadcast(P))
+        gain = const.tile([P, 2, HEAD_DIM], BF16, name="gain")
+        nc.scalar.dma_start(out=gain[:, 0, :], in_=q_scale_vid.partition_broadcast(P))
+        nc.scalar.dma_start(out=gain[:, 1, :], in_=k_scale_vid.partition_broadcast(P))
+        eps = const.tile([P, 1], F32, name="eps")
+        nc.vector.memset(eps[:], EPS)
+        squares = const.tile([P, HEAD_DIM], F32, name="squares")
+
+        ident = const.tile([P, P], F32, name="ident")
+        make_identity(nc, ident[:])
+        perm = const.tile([P, P], F32, name="perm")
+        nc.vector.tensor_copy(
+            out=perm[:].rearrange("p (a w l) -> p a w l", a=4, w=4, l=WIN_SIDE),
+            in_=ident[:].rearrange("p (a l w) -> p a w l", a=4, l=WIN_SIDE, w=4),
+        )
+
+        for r in range(1, LEAD):
+            load_round(r)
+
+        def transpose_round(r):
+            words = x_of[r][:].bitcast(F32).rearrange("p (j g q u) -> p j g u q", j=ROUND, g=PASSES, q=P, u=2)
+            grouped = grouped_pool.tile([P, ROUND * K], BF16, name="grouped", align_bytes=64)
+            grouped_words = grouped[:].bitcast(F32).rearrange("p (j g m u) -> p j g m u", j=ROUND, g=PASSES, m=P, u=2)
+            for j in range(ROUND):
+                xt = xt_psum.tile([P, PASSES, 2, P], F32, name="xt")
+                for g in range(PASSES):
+                    for u in range(2):
+                        nc.tensor.transpose(xt[:, g, u, :], words[:, j, g, u, :], perm[:])
+                nc.scalar.copy(out=grouped_words[:, j], in_=xt[:].rearrange("p g u m -> p g m u"))
+            grouped_of[r] = grouped
+
+        def quantise_round(r):
+            codes = code_pool.tile([P, ROUND * PASSES * P], U32, name="codes", align_bytes=64)
+            x_scales = code_pool.tile([P, ROUND * PASSES * P], U8, name="x_scales", align_bytes=64)
+            nc.vector.quantize_mx(out=codes[:].bitcast(FP8X4), scales=x_scales[:], in_=grouped_of[r][:])
+            codes_of[r] = (codes, x_scales)
+
+        def project_round(r):
+            codes, x_scales = codes_of[r]
+            y = y_pool.tile([P, QKV, ROUND, INNER], F32, name="y")
+            for j in range(ROUND):
+                acc = acc_psum.tile([P, QKV, INNER], F32, name="acc")
+                for c in range(QKV):
+                    for g in range(PASSES):
+                        tokens = slice((j * PASSES + g) * P, (j * PASSES + g + 1) * P)
+                        nc.tensor.matmul_mx(
+                            out=acc[:, c, :],
+                            lhsT=codes[:, tokens].bitcast(FP8X4),
+                            lhsT_scale=x_scales[:, tokens],
+                            rhs=w_words[:, g, 2 * c * INNER : 2 * (c + 1) * INNER].bitcast(FP4X4),
+                            rhs_scale=w_scales[:, g, c * INNER : (c + 1) * INNER],
+                            start=(g == 0),
+                            stop=(g == PASSES - 1),
+                        )
+                nc.vector.tensor_tensor(out=y[:, :, j, :], in0=acc[:], in1=bias[:], op=ALU.add)
+            y_of[r] = y
+
+        def normalise_and_store_round(r):
+            y = y_of[r]
+            sum_sq = stat_pool.tile([P, 2, ROUND, HEADS], F32, name="sum_sq")
+            rstd = stat_pool.tile([P, 2, ROUND, HEADS], F32, name="rstd")
+            for c in range(2):
+                for j in range(ROUND):
+                    for h in range(HEADS):
+                        nc.scalar.activation(
+                            out=squares[:],
+                            in_=y[:, c, j, h * HEAD_DIM : (h + 1) * HEAD_DIM],
+                            func=ACT.Square,
+                            accum_out=sum_sq[:, c, j, h : h + 1],
+                        )
+            nc.scalar.activation(
+                out=rstd[:], in_=sum_sq[:], func=ACT.Abs_reciprocal_sqrt, scale=1.0 / HEAD_DIM, bias=eps[:, 0:1]
+            )
+            for c in range(2):
+                for j in range(ROUND):
+                    for h in range(HEADS):
+                        head = y[:, c, j, h * HEAD_DIM : (h + 1) * HEAD_DIM]
+                        nc.vector.scalar_tensor_tensor(
+                            out=head, in0=head, scalar=rstd[:, c, j, h : h + 1], in1=gain[:, c, :], op0=ALU.mult, op1=ALU.mult
+                        )
+            frame, part = divmod(r, ROUNDS_PER_FRAME)
+            for c in range(QKV):
+                nc.sync.dma_start(
+                    out=outs_by_frame[c][frame, :, :, part * ROUND * INNER : (part + 1) * ROUND * INNER],
+                    in_=y[:, c].rearrange("p j f -> p (j f)"),
+                )
+
+        transpose_round(0)
+        for i in range(ROUNDS + 2):
+            if i < ROUNDS:
+                quantise_round(i)
+            if 0 <= i - 1 < ROUNDS:
+                project_round(i - 1)
+            if 0 <= i - 2 < ROUNDS:
+                normalise_and_store_round(i - 2)
+            if i + LEAD < ROUNDS:
+                load_round(i + LEAD)
+            if i + 1 < ROUNDS:
+                transpose_round(i + 1)

@@ -53,6 +53,7 @@ def tile_naswinattention_pa_t_kernel(
         code_pool = stack.enter_context(tc.tile_pool(name="code_pool", bufs=3))
         y_pool = stack.enter_context(tc.tile_pool(name="y_pool", bufs=4))
         stat_pool = stack.enter_context(tc.tile_pool(name="stat_pool", bufs=4))
+        squares_pool = stack.enter_context(tc.tile_pool(name="squares_pool", bufs=2))
         xt_psum = stack.enter_context(tc.psum_pool(name="xt_psum", bufs=4))
         acc_psum = stack.enter_context(tc.psum_pool(name="acc_psum", bufs=4))
 
@@ -87,7 +88,6 @@ def tile_naswinattention_pa_t_kernel(
         nc.scalar.dma_start(out=gain[:, 1, :], in_=k_scale_vid.partition_broadcast(P))
         eps = const.tile([P, 1], F32, name="eps")
         nc.vector.memset(eps[:], EPS)
-        squares = const.tile([P, HEAD_DIM], F32, name="squares")
 
         ident = const.tile([P, P], F32, name="ident")
         make_identity(nc, ident[:])
@@ -142,11 +142,12 @@ def tile_naswinattention_pa_t_kernel(
             y = y_of[r]
             sum_sq = stat_pool.tile([P, 2, ROUND, HEADS], F32, name="sum_sq")
             rstd = stat_pool.tile([P, 2, ROUND, HEADS], F32, name="rstd")
+            squares = squares_pool.tile([P, 2, ROUND, INNER], BF16, name="squares")
             for c in range(2):
                 for j in range(ROUND):
                     for h in range(HEADS):
                         nc.scalar.activation(
-                            out=squares[:],
+                            out=squares[:, c, j, h * HEAD_DIM : (h + 1) * HEAD_DIM],
                             in_=y[:, c, j, h * HEAD_DIM : (h + 1) * HEAD_DIM],
                             func=ACT.Square,
                             accum_out=sum_sq[:, c, j, h : h + 1],

@@ -21,17 +21,20 @@ HEADS = 2
 HEAD_DIM = 64
 INNER = HEADS * HEAD_DIM
 QKV = 3
+NORMED = 2
 EPS = 1e-6
 
 FRAMES = 8
-WINDOWS = 16
 WIN_SIDE = 8
-TOKENS = FRAMES * WINDOWS * WIN_SIDE * WIN_SIDE
+TOKENS = FRAMES * P * WIN_SIDE
 
-ROUND = 4
-ROUNDS_PER_FRAME = WIN_SIDE // ROUND
-ROUNDS = FRAMES * ROUNDS_PER_FRAME
-LEAD = 6
+CHUNK = 4
+CHUNKS_PER_FRAME = WIN_SIDE // CHUNK
+CHUNKS = FRAMES * CHUNKS_PER_FRAME
+ROUND = 2
+ROUNDS_PER_CHUNK = CHUNK // ROUND
+ROUNDS = CHUNKS * ROUNDS_PER_CHUNK
+X_BUFS = 6
 
 FLOPS = 2 * TOKENS * K * QKV * INNER
 
@@ -48,29 +51,44 @@ def tile_naswinattention_pa_t_kernel(
 
     with ExitStack() as stack:
         const = stack.enter_context(tc.tile_pool(name="const", bufs=1))
-        x_pool = stack.enter_context(tc.tile_pool(name="x_pool", bufs=LEAD))
-        grouped_pool = stack.enter_context(tc.tile_pool(name="grouped_pool", bufs=2))
+        x_pool = stack.enter_context(tc.tile_pool(name="x_pool", bufs=X_BUFS))
+        grouped_pool = stack.enter_context(tc.tile_pool(name="grouped_pool", bufs=3))
         code_pool = stack.enter_context(tc.tile_pool(name="code_pool", bufs=3))
         y_pool = stack.enter_context(tc.tile_pool(name="y_pool", bufs=4))
         stat_pool = stack.enter_context(tc.tile_pool(name="stat_pool", bufs=4))
         squares_pool = stack.enter_context(tc.tile_pool(name="squares_pool", bufs=2))
-        xt_psum = stack.enter_context(tc.psum_pool(name="xt_psum", bufs=4))
-        acc_psum = stack.enter_context(tc.psum_pool(name="acc_psum", bufs=4))
-
+        xt_psum = stack.enter_context(tc.psum_pool(name="xt_psum", bufs=2 * ROUND))
+        acc_psum = stack.enter_context(tc.psum_pool(name="acc_psum", bufs=2 * ROUND))
         stack.enter_context(tc.manual_schedule())
 
         x_of = {}
+        y_of = {}
+        xt_of = {}
         grouped_of = {}
         codes_of = {}
-        y_of = {}
+        acc_of = {}
+        sum_sq_of = {}
+        rstd_of = {}
 
-        def load_round(r):
-            frame, part = divmod(r, ROUNDS_PER_FRAME)
-            x = x_pool.tile([P, ROUND * K], BF16, name="x")
-            nc.sync.dma_start(out=x[:], in_=vid_by_frame[frame, :, part * ROUND * K : (part + 1) * ROUND * K])
-            x_of[r] = x
+        def load_chunk(chunk, pieces):
+            frame, part = divmod(chunk, CHUNKS_PER_FRAME)
+            x = x_pool.tile([P, CHUNK * K], BF16, name="x")
+            width = CHUNK * K // pieces
+            for piece in range(pieces):
+                nc.sync.dma_start(
+                    out=x[:, piece * width : (piece + 1) * width],
+                    in_=vid_by_frame[frame, :, part * CHUNK * K + piece * width : part * CHUNK * K + (piece + 1) * width],
+                )
+            x_of[chunk] = x
 
-        load_round(0)
+        def store_chunk(chunk, c):
+            frame, part = divmod(chunk, CHUNKS_PER_FRAME)
+            nc.sync.dma_start(
+                out=outs_by_frame[c][frame, :, :, part * CHUNK * INNER : (part + 1) * CHUNK * INNER],
+                in_=y_of[chunk][:, c].rearrange("p j f -> p (j f)"),
+            )
+
+        load_chunk(0, CHUNK)
 
         w_words = const.tile([P, PASSES, 2 * QKV * INNER], U8, name="w_words", align_bytes=64)
         nc.sync.dma_start(out=w_words[:].bitcast(I32), in_=Wqkv_vid_words.bitcast(I32).rearrange("g p n -> p g n"))
@@ -81,11 +99,16 @@ def tile_naswinattention_pa_t_kernel(
                 out=w_scales[32 * quadrant : 32 * quadrant + 4].bitcast(I32),
                 in_=Wqkv_vid_scales.bitcast(I32)[:, 4 * quadrant : 4 * quadrant + 4, :].rearrange("g r n -> r g n"),
             )
-        bias = const.tile([P, QKV, INNER], BF16, name="bias")
-        nc.scalar.dma_start(out=bias[:].rearrange("p c f -> p (c f)"), in_=bqkv_vid.partition_broadcast(P))
-        gain = const.tile([P, 2, HEAD_DIM], BF16, name="gain")
-        nc.scalar.dma_start(out=gain[:, 0, :], in_=q_scale_vid.partition_broadcast(P))
-        nc.scalar.dma_start(out=gain[:, 1, :], in_=k_scale_vid.partition_broadcast(P))
+
+        row_width = (QKV + 1) * INNER
+        gain_at = QKV * INNER
+        rows = const.tile([P, row_width], BF16, name="rows")
+        nc.vector.memset(rows[:], 0.0)
+        nc.scalar.dma_start(out=rows[0:1, 0:gain_at], in_=bqkv_vid.unsqueeze(0))
+        nc.scalar.dma_start(out=rows[0:1, gain_at : gain_at + HEAD_DIM], in_=q_scale_vid.unsqueeze(0))
+        nc.scalar.dma_start(out=rows[0:1, gain_at + HEAD_DIM : row_width], in_=k_scale_vid.unsqueeze(0))
+        ones = const.tile([P, P], BF16, name="ones")
+        nc.vector.memset(ones[:], 1.0)
         eps = const.tile([P, 1], F32, name="eps")
         nc.vector.memset(eps[:], EPS)
 
@@ -97,20 +120,31 @@ def tile_naswinattention_pa_t_kernel(
             in_=ident[:].rearrange("p (a l w) -> p a w l", a=4, l=WIN_SIDE, w=4),
         )
 
-        for r in range(1, LEAD):
-            load_round(r)
+        spread = acc_psum.tile([P, row_width], F32, name="spread", tag="acc")
+        nc.tensor.matmul(out=spread[:], lhsT=ones[:], rhs=rows[:], start=True, stop=True)
+        on_all = const.tile([P, row_width], F32, name="on_all")
+        nc.vector.tensor_copy(out=on_all[:], in_=spread[:])
+        bias = on_all[:, 0:gain_at].rearrange("p (c f) -> p c f", c=QKV)
+        gain = on_all[:, gain_at:row_width].rearrange("p (c f) -> p c f", c=NORMED)
+
+        for chunk in range(1, X_BUFS):
+            load_chunk(chunk, 1)
 
         def transpose_round(r):
-            words = x_of[r][:].bitcast(F32).rearrange("p (j g q u) -> p j g u q", j=ROUND, g=PASSES, q=P, u=2)
-            grouped = grouped_pool.tile([P, ROUND * K], BF16, name="grouped", align_bytes=64)
-            grouped_words = grouped[:].bitcast(F32).rearrange("p (j g m u) -> p j g m u", j=ROUND, g=PASSES, m=P, u=2)
+            chunk, part = divmod(r, ROUNDS_PER_CHUNK)
+            words = x_of[chunk][:].bitcast(F32).rearrange("p (j g q u) -> p j g u q", j=CHUNK, g=PASSES, q=P, u=2)
+            xt_of[r] = []
             for j in range(ROUND):
                 xt = xt_psum.tile([P, PASSES, 2, P], F32, name="xt")
                 for g in range(PASSES):
                     for u in range(2):
-                        nc.tensor.transpose(xt[:, g, u, :], words[:, j, g, u, :], perm[:])
-                nc.scalar.copy(out=grouped_words[:, j], in_=xt[:].rearrange("p g u m -> p g m u"))
-            grouped_of[r] = grouped
+                        nc.tensor.transpose(xt[:, g, u, :], words[:, part * ROUND + j, g, u, :], perm[:])
+                xt_of[r].append(xt)
+            grouped_of[r] = grouped_pool.tile([P, ROUND * K], BF16, name="grouped", align_bytes=64)
+
+        def regroup_tile(r, j):
+            grouped_words = grouped_of[r][:].bitcast(F32).rearrange("p (j g m u) -> p j g m u", j=ROUND, g=PASSES, m=P, u=2)
+            nc.scalar.copy(out=grouped_words[:, j], in_=xt_of[r][j][:].rearrange("p g u m -> p g m u"))
 
         def quantise_round(r):
             codes = code_pool.tile([P, ROUND * PASSES * P], U32, name="codes", align_bytes=64)
@@ -120,7 +154,7 @@ def tile_naswinattention_pa_t_kernel(
 
         def project_round(r):
             codes, x_scales = codes_of[r]
-            y = y_pool.tile([P, QKV, ROUND, INNER], F32, name="y")
+            acc_of[r] = []
             for j in range(ROUND):
                 acc = acc_psum.tile([P, QKV, INNER], F32, name="acc")
                 for c in range(QKV):
@@ -135,49 +169,78 @@ def tile_naswinattention_pa_t_kernel(
                             start=(g == 0),
                             stop=(g == PASSES - 1),
                         )
-                nc.vector.tensor_tensor(out=y[:, :, j, :], in0=acc[:], in1=bias[:], op=ALU.add)
-            y_of[r] = y
+                acc_of[r].append(acc)
 
-        def normalise_and_store_round(r):
-            y = y_of[r]
-            sum_sq = stat_pool.tile([P, 2, ROUND, HEADS], F32, name="sum_sq")
-            rstd = stat_pool.tile([P, 2, ROUND, HEADS], F32, name="rstd")
-            squares = squares_pool.tile([P, 2, ROUND, INNER], BF16, name="squares")
-            for c in range(2):
-                for j in range(ROUND):
-                    for h in range(HEADS):
-                        nc.scalar.activation(
-                            out=squares[:, c, j, h * HEAD_DIM : (h + 1) * HEAD_DIM],
-                            in_=y[:, c, j, h * HEAD_DIM : (h + 1) * HEAD_DIM],
-                            func=ACT.Square,
-                            accum_out=sum_sq[:, c, j, h : h + 1],
-                        )
-            nc.scalar.activation(
-                out=rstd[:], in_=sum_sq[:], func=ACT.Abs_reciprocal_sqrt, scale=1.0 / HEAD_DIM, bias=eps[:, 0:1]
-            )
-            for c in range(2):
-                for j in range(ROUND):
-                    for h in range(HEADS):
-                        head = y[:, c, j, h * HEAD_DIM : (h + 1) * HEAD_DIM]
-                        nc.vector.scalar_tensor_tensor(
-                            out=head, in0=head, scalar=rstd[:, c, j, h : h + 1], in1=gain[:, c, :], op0=ALU.mult, op1=ALU.mult
-                        )
-            frame, part = divmod(r, ROUNDS_PER_FRAME)
-            for c in range(QKV):
-                nc.sync.dma_start(
-                    out=outs_by_frame[c][frame, :, :, part * ROUND * INNER : (part + 1) * ROUND * INNER],
-                    in_=y[:, c].rearrange("p j f -> p (j f)"),
+        def add_bias_round(r):
+            chunk, part = divmod(r, ROUNDS_PER_CHUNK)
+            if part == 0:
+                y_of[chunk] = y_pool.tile([P, QKV, CHUNK, INNER], F32, name="y")
+            for j in range(ROUND):
+                nc.vector.tensor_tensor(out=y_of[chunk][:, :, part * ROUND + j, :], in0=acc_of[r][j][:], in1=bias, op=ALU.add)
+            if part == ROUNDS_PER_CHUNK - 1:
+                store_chunk(chunk, QKV - 1)
+
+        def heads_of_round(r):
+            chunk, part = divmod(r, ROUNDS_PER_CHUNK)
+            return [
+                (c, j, h, y_of[chunk][:, c, part * ROUND + j, h * HEAD_DIM : (h + 1) * HEAD_DIM])
+                for c in range(NORMED)
+                for j in range(ROUND)
+                for h in range(HEADS)
+            ]
+
+        def sum_squares_round(r):
+            sum_sq_of[r] = stat_pool.tile([P, NORMED, ROUND, HEADS], F32, name="sum_sq")
+            squares = squares_pool.tile([P, NORMED, ROUND, INNER], BF16, name="squares")
+            for c, j, h, head in heads_of_round(r):
+                nc.scalar.activation(
+                    out=squares[:, c, j, h * HEAD_DIM : (h + 1) * HEAD_DIM],
+                    in_=head,
+                    func=ACT.Square,
+                    accum_out=sum_sq_of[r][:, c, j, h : h + 1],
                 )
 
-        transpose_round(0)
-        for i in range(ROUNDS + 2):
-            if i < ROUNDS:
+        def inverse_rms_round(r):
+            rstd_of[r] = stat_pool.tile([P, NORMED, ROUND, HEADS], F32, name="rstd")
+            nc.scalar.activation(
+                out=rstd_of[r][:], in_=sum_sq_of[r][:], func=ACT.Abs_reciprocal_sqrt, scale=1.0 / HEAD_DIM, bias=eps[:, 0:1]
+            )
+
+        def scale_round(r):
+            for c, j, h, head in heads_of_round(r):
+                nc.vector.scalar_tensor_tensor(
+                    out=head, in0=head, scalar=rstd_of[r][:, c, j, h : h + 1], in1=gain[:, c, :], op0=ALU.mult, op1=ALU.mult
+                )
+            chunk, part = divmod(r, ROUNDS_PER_CHUNK)
+            if part == ROUNDS_PER_CHUNK - 1:
+                for c in range(NORMED):
+                    store_chunk(chunk, c)
+
+        def is_round(r):
+            return 0 <= r < ROUNDS
+
+        for i in range(-2, ROUNDS + 4):
+            if is_round(i - 2):
+                add_bias_round(i - 2)
+            if is_round(i):
                 quantise_round(i)
-            if 0 <= i - 1 < ROUNDS:
+            if is_round(i - 3):
+                scale_round(i - 3)
+
+            if is_round(i + 1):
+                regroup_tile(i + 1, 0)
+            if is_round(i - 2):
+                sum_squares_round(i - 2)
+            if is_round(i + 1):
+                for j in range(1, ROUND):
+                    regroup_tile(i + 1, j)
+            if is_round(i - 2):
+                inverse_rms_round(i - 2)
+
+            if is_round(i - 1):
                 project_round(i - 1)
-            if 0 <= i - 2 < ROUNDS:
-                normalise_and_store_round(i - 2)
-            if i + LEAD < ROUNDS:
-                load_round(i + LEAD)
-            if i + 1 < ROUNDS:
-                transpose_round(i + 1)
+            if is_round(i + 2):
+                transpose_round(i + 2)
+                chunk, part = divmod(i + 2, ROUNDS_PER_CHUNK)
+                if part == ROUNDS_PER_CHUNK - 1 and chunk + X_BUFS < CHUNKS:
+                    load_chunk(chunk + X_BUFS, 1)

@@ -88,7 +88,27 @@ def tile_naswinattention_pa_t_kernel(
                 in_=y_of[chunk][:, c].rearrange("p j f -> p (j f)"),
             )
 
+
+        row_width = (QKV + 1) * INNER
+        gain_at = QKV * INNER
+        rows = const.tile([P, row_width], BF16, name="rows")
+        nc.vector.memset(rows[:], 0.0)
+        nc.scalar.dma_start(out=rows[0:1, 0:gain_at], in_=bqkv_vid.unsqueeze(0))
+        nc.scalar.dma_start(out=rows[0:1, gain_at : gain_at + HEAD_DIM], in_=q_scale_vid.unsqueeze(0))
+        nc.scalar.dma_start(out=rows[0:1, gain_at + HEAD_DIM : row_width], in_=k_scale_vid.unsqueeze(0))
+        ones = const.tile([P, P], BF16, name="ones")
+        nc.vector.memset(ones[:], 1.0)
+        bias = const.tile([P, QKV, INNER], F32, name="bias")
+        gain = const.tile([P, NORMED, HEAD_DIM], BF16, name="gain")
+
+        def spread_rows():
+            spread = acc_psum.tile([P, row_width], F32, name="spread", tag="acc")
+            nc.tensor.matmul(out=spread[:], lhsT=ones[:], rhs=rows[:], start=True, stop=True)
+            nc.vector.tensor_copy(out=bias[:], in_=spread[:, 0:gain_at].rearrange("p (c f) -> p c f", c=QKV))
+            nc.vector.tensor_copy(out=gain[:], in_=spread[:, gain_at:row_width].rearrange("p (c f) -> p c f", c=NORMED))
+
         load_chunk(0, CHUNK)
+        load_chunk(1, 1)
 
         w_words = const.tile([P, PASSES, 2 * QKV * INNER], U8, name="w_words", align_bytes=64)
         nc.sync.dma_start(out=w_words[:].bitcast(I32), in_=Wqkv_vid_words.bitcast(I32).rearrange("g p n -> p g n"))
@@ -100,17 +120,13 @@ def tile_naswinattention_pa_t_kernel(
                 in_=Wqkv_vid_scales.bitcast(I32)[:, 4 * quadrant : 4 * quadrant + 4, :].rearrange("g r n -> r g n"),
             )
 
-        row_width = (QKV + 1) * INNER
-        gain_at = QKV * INNER
-        rows = const.tile([P, row_width], BF16, name="rows")
-        nc.vector.memset(rows[:], 0.0)
-        nc.scalar.dma_start(out=rows[0:1, 0:gain_at], in_=bqkv_vid.unsqueeze(0))
-        nc.scalar.dma_start(out=rows[0:1, gain_at : gain_at + HEAD_DIM], in_=q_scale_vid.unsqueeze(0))
-        nc.scalar.dma_start(out=rows[0:1, gain_at + HEAD_DIM : row_width], in_=k_scale_vid.unsqueeze(0))
-        ones = const.tile([P, P], BF16, name="ones")
-        nc.vector.memset(ones[:], 1.0)
+        for chunk in range(2, X_BUFS):
+            load_chunk(chunk, 1)
+
         eps = const.tile([P, 1], F32, name="eps")
         nc.vector.memset(eps[:], EPS)
+        table_warmer = const.tile([P, 1], F32, name="table_warmer")
+        nc.scalar.activation(out=table_warmer[:], in_=eps[:], func=ACT.Abs_reciprocal_sqrt)
 
         ident = const.tile([P, P], F32, name="ident")
         make_identity(nc, ident[:])
@@ -119,16 +135,6 @@ def tile_naswinattention_pa_t_kernel(
             out=perm[:].rearrange("p (a w l) -> p a w l", a=4, w=4, l=WIN_SIDE),
             in_=ident[:].rearrange("p (a l w) -> p a w l", a=4, l=WIN_SIDE, w=4),
         )
-
-        spread = acc_psum.tile([P, row_width], F32, name="spread", tag="acc")
-        nc.tensor.matmul(out=spread[:], lhsT=ones[:], rhs=rows[:], start=True, stop=True)
-        on_all = const.tile([P, row_width], F32, name="on_all")
-        nc.vector.tensor_copy(out=on_all[:], in_=spread[:])
-        bias = on_all[:, 0:gain_at].rearrange("p (c f) -> p c f", c=QKV)
-        gain = on_all[:, gain_at:row_width].rearrange("p (c f) -> p c f", c=NORMED)
-
-        for chunk in range(1, X_BUFS):
-            load_chunk(chunk, 1)
 
         def transpose_round(r):
             chunk, part = divmod(r, ROUNDS_PER_CHUNK)
@@ -176,7 +182,7 @@ def tile_naswinattention_pa_t_kernel(
             if part == 0:
                 y_of[chunk] = y_pool.tile([P, QKV, CHUNK, INNER], F32, name="y")
             for j in range(ROUND):
-                nc.vector.tensor_tensor(out=y_of[chunk][:, :, part * ROUND + j, :], in0=acc_of[r][j][:], in1=bias, op=ALU.add)
+                nc.vector.tensor_tensor(out=y_of[chunk][:, :, part * ROUND + j, :], in0=acc_of[r][j][:], in1=bias[:], op=ALU.add)
             if part == ROUNDS_PER_CHUNK - 1:
                 store_chunk(chunk, QKV - 1)
 
@@ -207,19 +213,20 @@ def tile_naswinattention_pa_t_kernel(
             )
 
         def scale_round(r):
+            chunk, part = divmod(r, ROUNDS_PER_CHUNK)
             for c, j, h, head in heads_of_round(r):
                 nc.vector.scalar_tensor_tensor(
                     out=head, in0=head, scalar=rstd_of[r][:, c, j, h : h + 1], in1=gain[:, c, :], op0=ALU.mult, op1=ALU.mult
                 )
-            chunk, part = divmod(r, ROUNDS_PER_CHUNK)
-            if part == ROUNDS_PER_CHUNK - 1:
-                for c in range(NORMED):
+                if part == ROUNDS_PER_CHUNK - 1 and j == ROUND - 1 and h == HEADS - 1:
                     store_chunk(chunk, c)
 
         def is_round(r):
             return 0 <= r < ROUNDS
 
-        for i in range(-2, ROUNDS + 4):
+        transpose_round(0)
+        spread_rows()
+        for i in range(-1, ROUNDS + 4):
             if is_round(i - 2):
                 add_bias_round(i - 2)
             if is_round(i):

@@ -70,16 +70,17 @@ def tile_naswinattention_pa_t_kernel(
         sum_sq_of = {}
         rstd_of = {}
 
-        def load_chunk(chunk, pieces):
+        def load_tiles(chunk, first, tiles):
             frame, part = divmod(chunk, CHUNKS_PER_FRAME)
-            x = x_pool.tile([P, CHUNK * K], BF16, name="x")
-            width = CHUNK * K // pieces
-            for piece in range(pieces):
-                nc.sync.dma_start(
-                    out=x[:, piece * width : (piece + 1) * width],
-                    in_=vid_by_frame[frame, :, part * CHUNK * K + piece * width : part * CHUNK * K + (piece + 1) * width],
-                )
-            x_of[chunk] = x
+            if first == 0:
+                x_of[chunk] = x_pool.tile([P, CHUNK * K], BF16, name="x")
+            nc.sync.dma_start(
+                out=x_of[chunk][:, first * K : (first + tiles) * K],
+                in_=vid_by_frame[frame, :, (part * CHUNK + first) * K : (part * CHUNK + first + tiles) * K],
+            )
+
+        def load_chunk(chunk):
+            load_tiles(chunk, 0, CHUNK)
 
         def store_chunk(chunk, c):
             frame, part = divmod(chunk, CHUNKS_PER_FRAME)
@@ -107,8 +108,10 @@ def tile_naswinattention_pa_t_kernel(
             nc.vector.tensor_copy(out=bias[:], in_=spread[:, 0:gain_at].rearrange("p (c f) -> p c f", c=QKV))
             nc.vector.tensor_copy(out=gain[:], in_=spread[:, gain_at:row_width].rearrange("p (c f) -> p c f", c=NORMED))
 
-        load_chunk(0, CHUNK)
-        load_chunk(1, 1)
+        for j in range(CHUNK):
+            load_tiles(0, j, 1)
+        for j in range(ROUND):
+            load_tiles(1, j, 1)
 
         w_words = const.tile([P, PASSES, 2 * QKV * INNER], U8, name="w_words", align_bytes=64)
         nc.sync.dma_start(out=w_words[:].bitcast(I32), in_=Wqkv_vid_words.bitcast(I32).rearrange("g p n -> p g n"))
@@ -120,8 +123,9 @@ def tile_naswinattention_pa_t_kernel(
                 in_=Wqkv_vid_scales.bitcast(I32)[:, 4 * quadrant : 4 * quadrant + 4, :].rearrange("g r n -> r g n"),
             )
 
+        load_tiles(1, ROUND, CHUNK - ROUND)
         for chunk in range(2, X_BUFS):
-            load_chunk(chunk, 1)
+            load_chunk(chunk)
 
         eps = const.tile([P, 1], F32, name="eps")
         nc.vector.memset(eps[:], EPS)
@@ -250,4 +254,4 @@ def tile_naswinattention_pa_t_kernel(
                 transpose_round(i + 2)
                 chunk, part = divmod(i + 2, ROUNDS_PER_CHUNK)
                 if part == ROUNDS_PER_CHUNK - 1 and chunk + X_BUFS < CHUNKS:
-                    load_chunk(chunk + X_BUFS, 1)
+                    load_chunk(chunk + X_BUFS)

@@ -69,25 +69,33 @@ def tile_naswinattention_pa_t_kernel(
         acc_of = {}
         sum_sq_of = {}
         rstd_of = {}
+        squares_of = {}
+        spread_of = []
 
-        def load_tiles(chunk, first, tiles):
+        def load_columns(chunk, first, columns):
             frame, part = divmod(chunk, CHUNKS_PER_FRAME)
             if first == 0:
                 x_of[chunk] = x_pool.tile([P, CHUNK * K], BF16, name="x")
             nc.sync.dma_start(
-                out=x_of[chunk][:, first * K : (first + tiles) * K],
-                in_=vid_by_frame[frame, :, (part * CHUNK + first) * K : (part * CHUNK + first + tiles) * K],
+                out=x_of[chunk][:, first : first + columns],
+                in_=vid_by_frame[frame, :, part * CHUNK * K + first : part * CHUNK * K + first + columns],
             )
+
+        def load_tiles(chunk, first, tiles):
+            load_columns(chunk, first * K, tiles * K)
 
         def load_chunk(chunk):
             load_tiles(chunk, 0, CHUNK)
 
-        def store_chunk(chunk, c):
+        def store_tiles(chunk, c, first, tiles):
             frame, part = divmod(chunk, CHUNKS_PER_FRAME)
             nc.sync.dma_start(
-                out=outs_by_frame[c][frame, :, :, part * CHUNK * INNER : (part + 1) * CHUNK * INNER],
-                in_=y_of[chunk][:, c].rearrange("p j f -> p (j f)"),
+                out=outs_by_frame[c][frame, :, :, (part * CHUNK + first) * INNER : (part * CHUNK + first + tiles) * INNER],
+                in_=y_of[chunk][:, c, first : first + tiles, :].rearrange("p j f -> p (j f)"),
             )
+
+        def store_chunk(chunk, c):
+            store_tiles(chunk, c, 0, CHUNK)
 
 
         row_width = (QKV + 1) * INNER
@@ -105,10 +113,15 @@ def tile_naswinattention_pa_t_kernel(
         def spread_rows():
             spread = acc_psum.tile([P, row_width], F32, name="spread", tag="acc")
             nc.tensor.matmul(out=spread[:], lhsT=ones[:], rhs=rows[:], start=True, stop=True)
+            return spread
+
+        def keep_rows(spread):
             nc.vector.tensor_copy(out=bias[:], in_=spread[:, 0:gain_at].rearrange("p (c f) -> p c f", c=QKV))
             nc.vector.tensor_copy(out=gain[:], in_=spread[:, gain_at:row_width].rearrange("p (c f) -> p c f", c=NORMED))
 
-        for j in range(CHUNK):
+        for g in range(PASSES):
+            load_columns(0, g * K_PASS, K_PASS)
+        for j in range(1, CHUNK):
             load_tiles(0, j, 1)
         for j in range(ROUND):
             load_tiles(1, j, 1)
@@ -190,63 +203,81 @@ def tile_naswinattention_pa_t_kernel(
             if part == ROUNDS_PER_CHUNK - 1:
                 store_chunk(chunk, QKV - 1)
 
-        def heads_of_round(r):
+        def heads_of_round(r, first, tiles):
             chunk, part = divmod(r, ROUNDS_PER_CHUNK)
             return [
                 (c, j, h, y_of[chunk][:, c, part * ROUND + j, h * HEAD_DIM : (h + 1) * HEAD_DIM])
                 for c in range(NORMED)
-                for j in range(ROUND)
+                for j in range(first, first + tiles)
                 for h in range(HEADS)
             ]
 
-        def sum_squares_round(r):
-            sum_sq_of[r] = stat_pool.tile([P, NORMED, ROUND, HEADS], F32, name="sum_sq")
-            squares = squares_pool.tile([P, NORMED, ROUND, INNER], BF16, name="squares")
-            for c, j, h, head in heads_of_round(r):
+        def sum_squares(r, first, tiles):
+            if first == 0:
+                sum_sq_of[r] = stat_pool.tile([P, NORMED, ROUND, HEADS], F32, name="sum_sq")
+                squares_of[r] = squares_pool.tile([P, NORMED, ROUND, INNER], BF16, name="squares")
+            for c, j, h, head in heads_of_round(r, first, tiles):
                 nc.scalar.activation(
-                    out=squares[:, c, j, h * HEAD_DIM : (h + 1) * HEAD_DIM],
+                    out=squares_of[r][:, c, j, h * HEAD_DIM : (h + 1) * HEAD_DIM],
                     in_=head,
                     func=ACT.Square,
                     accum_out=sum_sq_of[r][:, c, j, h : h + 1],
                 )
 
-        def inverse_rms_round(r):
-            rstd_of[r] = stat_pool.tile([P, NORMED, ROUND, HEADS], F32, name="rstd")
+        def inverse_rms(r, first, tiles):
+            if first == 0:
+                rstd_of[r] = stat_pool.tile([P, NORMED, ROUND, HEADS], F32, name="rstd")
             nc.scalar.activation(
-                out=rstd_of[r][:], in_=sum_sq_of[r][:], func=ACT.Abs_reciprocal_sqrt, scale=1.0 / HEAD_DIM, bias=eps[:, 0:1]
+                out=rstd_of[r][:, :, first : first + tiles, :],
+                in_=sum_sq_of[r][:, :, first : first + tiles, :],
+                func=ACT.Abs_reciprocal_sqrt,
+                scale=1.0 / HEAD_DIM,
+                bias=eps[:, 0:1],
             )
 
-        def scale_round(r):
+        def scale(r, first, tiles):
             chunk, part = divmod(r, ROUNDS_PER_CHUNK)
-            for c, j, h, head in heads_of_round(r):
+            for c, j, h, head in heads_of_round(r, first, tiles):
                 nc.vector.scalar_tensor_tensor(
                     out=head, in0=head, scalar=rstd_of[r][:, c, j, h : h + 1], in1=gain[:, c, :], op0=ALU.mult, op1=ALU.mult
                 )
-                if part == ROUNDS_PER_CHUNK - 1 and j == ROUND - 1 and h == HEADS - 1:
-                    store_chunk(chunk, c)
+                if j == ROUND - 1 and h == HEADS - 1:
+                    if chunk == CHUNKS - 1:
+                        store_tiles(chunk, c, part * ROUND, ROUND)
+                    elif part == ROUNDS_PER_CHUNK - 1:
+                        store_chunk(chunk, c)
+
+        def pieces_of(r):
+            return [(j, 1) for j in range(ROUND)] if r == ROUNDS - 1 else [(0, ROUND)]
 
         def is_round(r):
             return 0 <= r < ROUNDS
 
         transpose_round(0)
-        spread_rows()
         for i in range(-1, ROUNDS + 4):
             if is_round(i - 2):
                 add_bias_round(i - 2)
             if is_round(i):
                 quantise_round(i)
+            if i == 1:
+                keep_rows(spread_of[0])
             if is_round(i - 3):
-                scale_round(i - 3)
+                for first, tiles in pieces_of(i - 3):
+                    scale(i - 3, first, tiles)
 
             if is_round(i + 1):
                 regroup_tile(i + 1, 0)
             if is_round(i - 2):
-                sum_squares_round(i - 2)
+                for first, tiles in pieces_of(i - 2)[:-1]:
+                    sum_squares(i - 2, first, tiles)
+                    inverse_rms(i - 2, first, tiles)
+                first, tiles = pieces_of(i - 2)[-1]
+                sum_squares(i - 2, first, tiles)
             if is_round(i + 1):
                 for j in range(1, ROUND):
                     regroup_tile(i + 1, j)
             if is_round(i - 2):
-                inverse_rms_round(i - 2)
+                inverse_rms(i - 2, first, tiles)
 
             if is_round(i - 1):
                 project_round(i - 1)
@@ -255,3 +286,5 @@ def tile_naswinattention_pa_t_kernel(
                 chunk, part = divmod(i + 2, ROUNDS_PER_CHUNK)
                 if part == ROUNDS_PER_CHUNK - 1 and chunk + X_BUFS < CHUNKS:
                     load_chunk(chunk + X_BUFS)
+            if i == 0:
+                spread_of.append(spread_rows())

from contextlib import ExitStack

import concourse.mybir as mybir
from concourse.masks import make_identity

F32 = mybir.dt.float32
BF16 = mybir.dt.bfloat16
I32 = mybir.dt.int32
U32 = mybir.dt.uint32
U8 = mybir.dt.uint8
FP8X4 = mybir.dt.float8_e4m3fn_x4
FP4X4 = mybir.dt.float4_e2m1fn_x4
ACT = mybir.ActivationFunctionType
ALU = mybir.AluOpType

P = 128
K = 1024
K_PASS = 512
PASSES = K // K_PASS
HEADS = 2
HEAD_DIM = 64
INNER = HEADS * HEAD_DIM
QKV = 3
NORMED = 2
EPS = 1e-6

FRAMES = 8
WIN_SIDE = 8
TOKENS = FRAMES * P * WIN_SIDE

CHUNK = 4
CHUNKS_PER_FRAME = WIN_SIDE // CHUNK
CHUNKS = FRAMES * CHUNKS_PER_FRAME
ROUND = 2
ROUNDS_PER_CHUNK = CHUNK // ROUND
ROUNDS = CHUNKS * ROUNDS_PER_CHUNK
X_BUFS = 6

FLOPS = 2 * TOKENS * K * QKV * INNER


def tile_naswinattention_pa_t_kernel(
    tc, vid, Wqkv_vid_words, Wqkv_vid_scales, bqkv_vid, q_scale_vid, k_scale_vid, out_0, out_1, out_2
):
    nc = tc.nc

    vid_by_frame = vid.rearrange("(t p j) k -> t p (j k)", t=FRAMES, p=P, j=WIN_SIDE)
    outs_by_frame = [
        o.rearrange("n (t l j) h f -> t n l (j h f)", t=FRAMES, l=WIN_SIDE, j=WIN_SIDE) for o in (out_0, out_1, out_2)
    ]

    with ExitStack() as stack:
        const = stack.enter_context(tc.tile_pool(name="const", bufs=1))
        x_pool = stack.enter_context(tc.tile_pool(name="x_pool", bufs=X_BUFS))
        grouped_pool = stack.enter_context(tc.tile_pool(name="grouped_pool", bufs=3))
        code_pool = stack.enter_context(tc.tile_pool(name="code_pool", bufs=3))
        y_pool = stack.enter_context(tc.tile_pool(name="y_pool", bufs=4))
        stat_pool = stack.enter_context(tc.tile_pool(name="stat_pool", bufs=4))
        squares_pool = stack.enter_context(tc.tile_pool(name="squares_pool", bufs=2))
        xt_psum = stack.enter_context(tc.psum_pool(name="xt_psum", bufs=2 * ROUND))
        acc_psum = stack.enter_context(tc.psum_pool(name="acc_psum", bufs=2 * ROUND))
        stack.enter_context(tc.manual_schedule())

        x_of = {}
        y_of = {}
        xt_of = {}
        grouped_of = {}
        codes_of = {}
        acc_of = {}
        sum_sq_of = {}
        rstd_of = {}
        squares_of = {}
        spread_of = []

        def load_columns(chunk, first, columns):
            frame, part = divmod(chunk, CHUNKS_PER_FRAME)
            if first == 0:
                x_of[chunk] = x_pool.tile([P, CHUNK * K], BF16, name="x")
            nc.sync.dma_start(
                out=x_of[chunk][:, first : first + columns],
                in_=vid_by_frame[frame, :, part * CHUNK * K + first : part * CHUNK * K + first + columns],
            )

        def load_tiles(chunk, first, tiles):
            load_columns(chunk, first * K, tiles * K)

        def load_chunk(chunk):
            load_tiles(chunk, 0, CHUNK)

        def store_tiles(chunk, c, first, tiles):
            frame, part = divmod(chunk, CHUNKS_PER_FRAME)
            nc.sync.dma_start(
                out=outs_by_frame[c][frame, :, :, (part * CHUNK + first) * INNER : (part * CHUNK + first + tiles) * INNER],
                in_=y_of[chunk][:, c, first : first + tiles, :].rearrange("p j f -> p (j f)"),
            )

        def store_chunk(chunk, c):
            store_tiles(chunk, c, 0, CHUNK)


        row_width = (QKV + 1) * INNER
        gain_at = QKV * INNER
        rows = const.tile([P, row_width], BF16, name="rows")
        nc.vector.memset(rows[:], 0.0)
        nc.scalar.dma_start(out=rows[0:1, 0:gain_at], in_=bqkv_vid.unsqueeze(0))
        nc.scalar.dma_start(out=rows[0:1, gain_at : gain_at + HEAD_DIM], in_=q_scale_vid.unsqueeze(0))
        nc.scalar.dma_start(out=rows[0:1, gain_at + HEAD_DIM : row_width], in_=k_scale_vid.unsqueeze(0))
        ones = const.tile([P, P], BF16, name="ones")
        nc.vector.memset(ones[:], 1.0)
        bias = const.tile([P, QKV, INNER], F32, name="bias")
        gain = const.tile([P, NORMED, HEAD_DIM], BF16, name="gain")

        def spread_rows():
            spread = acc_psum.tile([P, row_width], F32, name="spread", tag="acc")
            nc.tensor.matmul(out=spread[:], lhsT=ones[:], rhs=rows[:], start=True, stop=True)
            return spread

        def keep_rows(spread):
            nc.vector.tensor_copy(out=bias[:], in_=spread[:, 0:gain_at].rearrange("p (c f) -> p c f", c=QKV))
            nc.vector.tensor_copy(out=gain[:], in_=spread[:, gain_at:row_width].rearrange("p (c f) -> p c f", c=NORMED))

        for g in range(PASSES):
            load_columns(0, g * K_PASS, K_PASS)
        for j in range(1, CHUNK):
            load_tiles(0, j, 1)
        for j in range(ROUND):
            load_tiles(1, j, 1)

        w_words = const.tile([P, PASSES, 2 * QKV * INNER], U8, name="w_words", align_bytes=64)
        nc.sync.dma_start(out=w_words[:].bitcast(I32), in_=Wqkv_vid_words.bitcast(I32).rearrange("g p n -> p g n"))
        w_scales = const.tile([P, PASSES, QKV * INNER], U8, name="w_scales", align_bytes=64)
        nc.vector.memset(w_scales[:].bitcast(I32), 0)
        for quadrant in range(4):
            nc.sync.dma_start(
                out=w_scales[32 * quadrant : 32 * quadrant + 4].bitcast(I32),
                in_=Wqkv_vid_scales.bitcast(I32)[:, 4 * quadrant : 4 * quadrant + 4, :].rearrange("g r n -> r g n"),
            )

        load_tiles(1, ROUND, CHUNK - ROUND)
        for chunk in range(2, X_BUFS):
            load_chunk(chunk)

        eps = const.tile([P, 1], F32, name="eps")
        nc.vector.memset(eps[:], EPS)
        table_warmer = const.tile([P, 1], F32, name="table_warmer")
        nc.scalar.activation(out=table_warmer[:], in_=eps[:], func=ACT.Abs_reciprocal_sqrt)

        ident = const.tile([P, P], F32, name="ident")
        make_identity(nc, ident[:])
        perm = const.tile([P, P], F32, name="perm")
        nc.vector.tensor_copy(
            out=perm[:].rearrange("p (a w l) -> p a w l", a=4, w=4, l=WIN_SIDE),
            in_=ident[:].rearrange("p (a l w) -> p a w l", a=4, l=WIN_SIDE, w=4),
        )

        def transpose_round(r):
            chunk, part = divmod(r, ROUNDS_PER_CHUNK)
            words = x_of[chunk][:].bitcast(F32).rearrange("p (j g q u) -> p j g u q", j=CHUNK, g=PASSES, q=P, u=2)
            xt_of[r] = []
            for j in range(ROUND):
                xt = xt_psum.tile([P, PASSES, 2, P], F32, name="xt")
                for g in range(PASSES):
                    for u in range(2):
                        nc.tensor.transpose(xt[:, g, u, :], words[:, part * ROUND + j, g, u, :], perm[:])
                xt_of[r].append(xt)
            grouped_of[r] = grouped_pool.tile([P, ROUND * K], BF16, name="grouped", align_bytes=64)

        def regroup_tile(r, j):
            grouped_words = grouped_of[r][:].bitcast(F32).rearrange("p (j g m u) -> p j g m u", j=ROUND, g=PASSES, m=P, u=2)
            nc.scalar.copy(out=grouped_words[:, j], in_=xt_of[r][j][:].rearrange("p g u m -> p g m u"))

        def quantise_round(r):
            codes = code_pool.tile([P, ROUND * PASSES * P], U32, name="codes", align_bytes=64)
            x_scales = code_pool.tile([P, ROUND * PASSES * P], U8, name="x_scales", align_bytes=64)
            nc.vector.quantize_mx(out=codes[:].bitcast(FP8X4), scales=x_scales[:], in_=grouped_of[r][:])
            codes_of[r] = (codes, x_scales)

        def project_round(r):
            codes, x_scales = codes_of[r]
            acc_of[r] = []
            for j in range(ROUND):
                acc = acc_psum.tile([P, QKV, INNER], F32, name="acc")
                for c in range(QKV):
                    for g in range(PASSES):
                        tokens = slice((j * PASSES + g) * P, (j * PASSES + g + 1) * P)
                        nc.tensor.matmul_mx(
                            out=acc[:, c, :],
                            lhsT=codes[:, tokens].bitcast(FP8X4),
                            lhsT_scale=x_scales[:, tokens],
                            rhs=w_words[:, g, 2 * c * INNER : 2 * (c + 1) * INNER].bitcast(FP4X4),
                            rhs_scale=w_scales[:, g, c * INNER : (c + 1) * INNER],
                            start=(g == 0),
                            stop=(g == PASSES - 1),
                        )
                acc_of[r].append(acc)

        def add_bias_round(r):
            chunk, part = divmod(r, ROUNDS_PER_CHUNK)
            if part == 0:
                y_of[chunk] = y_pool.tile([P, QKV, CHUNK, INNER], F32, name="y")
            for j in range(ROUND):
                nc.vector.tensor_tensor(out=y_of[chunk][:, :, part * ROUND + j, :], in0=acc_of[r][j][:], in1=bias[:], op=ALU.add)
            if part == ROUNDS_PER_CHUNK - 1:
                store_chunk(chunk, QKV - 1)

        def heads_of_round(r, first, tiles):
            chunk, part = divmod(r, ROUNDS_PER_CHUNK)
            return [
                (c, j, h, y_of[chunk][:, c, part * ROUND + j, h * HEAD_DIM : (h + 1) * HEAD_DIM])
                for c in range(NORMED)
                for j in range(first, first + tiles)
                for h in range(HEADS)
            ]

        def sum_squares(r, first, tiles):
            if first == 0:
                sum_sq_of[r] = stat_pool.tile([P, NORMED, ROUND, HEADS], F32, name="sum_sq")
                squares_of[r] = squares_pool.tile([P, NORMED, ROUND, INNER], BF16, name="squares")
            for c, j, h, head in heads_of_round(r, first, tiles):
                nc.scalar.activation(
                    out=squares_of[r][:, c, j, h * HEAD_DIM : (h + 1) * HEAD_DIM],
                    in_=head,
                    func=ACT.Square,
                    accum_out=sum_sq_of[r][:, c, j, h : h + 1],
                )

        def inverse_rms(r, first, tiles):
            if first == 0:
                rstd_of[r] = stat_pool.tile([P, NORMED, ROUND, HEADS], F32, name="rstd")
            nc.scalar.activation(
                out=rstd_of[r][:, :, first : first + tiles, :],
                in_=sum_sq_of[r][:, :, first : first + tiles, :],
                func=ACT.Abs_reciprocal_sqrt,
                scale=1.0 / HEAD_DIM,
                bias=eps[:, 0:1],
            )

        def scale(r, first, tiles):
            chunk, part = divmod(r, ROUNDS_PER_CHUNK)
            for c, j, h, head in heads_of_round(r, first, tiles):
                nc.vector.scalar_tensor_tensor(
                    out=head, in0=head, scalar=rstd_of[r][:, c, j, h : h + 1], in1=gain[:, c, :], op0=ALU.mult, op1=ALU.mult
                )
                if j == ROUND - 1 and h == HEADS - 1:
                    if chunk == CHUNKS - 1:
                        store_tiles(chunk, c, part * ROUND, ROUND)
                    elif part == ROUNDS_PER_CHUNK - 1:
                        store_chunk(chunk, c)

        def pieces_of(r):
            return [(j, 1) for j in range(ROUND)] if r == ROUNDS - 1 else [(0, ROUND)]

        def is_round(r):
            return 0 <= r < ROUNDS

        transpose_round(0)
        for i in range(-1, ROUNDS + 4):
            if is_round(i - 2):
                add_bias_round(i - 2)
            if is_round(i):
                quantise_round(i)
            if i == 1:
                keep_rows(spread_of[0])
            if is_round(i - 3):
                for first, tiles in pieces_of(i - 3):
                    scale(i - 3, first, tiles)

            if is_round(i + 1):
                regroup_tile(i + 1, 0)
            if is_round(i - 2):
                for first, tiles in pieces_of(i - 2)[:-1]:
                    sum_squares(i - 2, first, tiles)
                    inverse_rms(i - 2, first, tiles)
                first, tiles = pieces_of(i - 2)[-1]
                sum_squares(i - 2, first, tiles)
            if is_round(i + 1):
                for j in range(1, ROUND):
                    regroup_tile(i + 1, j)
            if is_round(i - 2):
                inverse_rms(i - 2, first, tiles)

            if is_round(i - 1):
                project_round(i - 1)
            if is_round(i + 2):
                transpose_round(i + 2)
                chunk, part = divmod(i + 2, ROUNDS_PER_CHUNK)
                if part == ROUNDS_PER_CHUNK - 1 and chunk + X_BUFS < CHUNKS:
                    load_chunk(chunk + X_BUFS)
            if i == 0:
                spread_of.append(spread_rows())
